import numpy as np
import ml_dtypes


def mxq(x, axis, fmt="e4m3"):
    dtype, down = {"e4m3": (ml_dtypes.float8_e4m3fn, 7), "e5m2": (ml_dtypes.float8_e5m2, 14)}[fmt]
    v = np.moveaxis(np.asarray(x, np.float32).astype(ml_dtypes.bfloat16).astype(np.float64), axis, -1)
    blocks = v.reshape(v.shape[:-1] + (-1, 32))
    amax = np.abs(blocks).max(-1, keepdims=True)
    byte = np.maximum(np.where(amax > 0, np.frexp(amax)[1] - 1 + 127, 0) - down, 1)
    scale = np.exp2(byte - 127.0)
    codes = (blocks / scale).astype(np.float32).astype(dtype).astype(np.float64)
    return np.moveaxis((codes * scale).reshape(v.shape), -1, axis)


WIDE = False


def mx_kscale(k):
    if not WIDE:
        return np.ones(k)
    levels = np.array([10, -10, 5, -5, 0])
    if k % 512:
        return np.exp2(np.random.permutation(np.resize(levels, k // 32))).repeat(32)
    a = np.empty((k // 512, 16))
    for p in range(k // 512):
        a[p, :8] = np.random.permutation(np.resize(levels, 8))
        for g in range(8):
            far = levels[np.abs(levels - a[p, g]) >= 10]
            a[p, g + 8] = far[np.random.randint(len(far))]
    return np.exp2(a.ravel()).repeat(32)


BF16 = ml_dtypes.bfloat16


def bf(x):
    return np.asarray(x, np.float32).astype(BF16)


def f64(x):
    return np.asarray(x).astype(np.float64)


NB, DI, DO, B = 8, 1024, 1024, 256
F = NB * DO
EPS = 1e-5


def setup_inputs():
    s, t = mx_kscale(DI), mx_kscale(F)
    tk = t.reshape(NB, DO)
    return {"x": bf(np.random.standard_normal((B, DI)) * s),
            "W": bf(np.random.standard_normal((NB, DI, DO)) / np.sqrt(DI) / s[None, :, None]),
            "b": bf(np.random.standard_normal((NB, DO)) * 0.5),
            "gamma": bf((1.0 + 0.2 * np.random.standard_normal((NB, DO))) * tk),
            "beta": bf(0.2 * np.random.standard_normal((NB, DO)) * tk),
            "Wf1": bf(np.random.standard_normal((F, DO)) / np.sqrt(F) / t[:, None]),
            "bf1": bf(np.random.standard_normal(DO) * 0.3)}


def reference(x, W, b, gamma, beta, Wf1, bf1):
    w2 = f64(W).transpose(1, 0, 2).reshape(DI, F)
    h = (mxq(f64(x), 1, "e4m3") @ mxq(w2, 0, "e4m3")).reshape(B, NB, DO) + f64(b)[None]
    h = np.maximum(h, 0.0)
    mean = h.mean(axis=0, keepdims=True)
    var = ((h - mean) ** 2).mean(axis=0, keepdims=True)
    h = (h - mean) * (1.0 / np.sqrt(var + EPS)) * f64(gamma)[None] + f64(beta)[None]
    fused = h.reshape(B, F)
    return np.maximum((mxq(fused, 1, "e4m3") @ mxq(f64(Wf1), 0, "e4m3")) + f64(bf1), 0.0)

@@ -1,0 +1,340 @@
+from contextlib import ExitStack
+
+import concourse.mybir as mybir
+from concourse.masks import make_identity
+
+F32 = mybir.dt.float32
+BF16 = mybir.dt.bfloat16
+U32 = mybir.dt.uint32
+U8 = mybir.dt.uint8
+FP8X4 = mybir.dt.float8_e4m3fn_x4
+ACT = mybir.ActivationFunctionType
+ALU = mybir.AluOpType
+
+P = 128
+PACK = 4
+K_PASS = P * PACK
+NB, DI, DO, B = 8, 1024, 1024, 256
+F = NB * DO
+EPS = 1e-5
+FLOPS = 2 * B * DI * F + 2 * B * F * DO
+
+TILES = DO // P
+GROUPS = DO // K_PASS
+W_PASSES = DI // K_PASS
+W_SLABS = NB * W_PASSES
+SLABS = W_SLABS + F // K_PASS
+ROUND_SLABS = 2
+ROUNDS = SLABS // ROUND_SLABS
+N_TILE = 512
+RUN = 4
+
+RAW_BUFS = 10
+BASE_COLS = 448
+RELU_SQUARES_COLS = 480
+NORMALISE_COLS = 128
+FUSED_COLS = 128
+
+
+def tile_extremeoptimizationlayer_pa_kernel(tc, x, W, b, gamma, beta, Wf1, bf1, out):
+    nc = tc.nc
+    with ExitStack() as ctx:
+        const = ctx.enter_context(tc.tile_pool(name="const", bufs=1))
+        raw_pool = ctx.enter_context(tc.tile_pool(name="raw", bufs=RAW_BUFS))
+        slab_pool = ctx.enter_context(tc.tile_pool(name="slab", bufs=2 * ROUND_SLABS))
+        branch_pool = ctx.enter_context(tc.tile_pool(name="branch", bufs=2))
+        result_pool = ctx.enter_context(tc.tile_pool(name="result", bufs=4))
+        psum_h = ctx.enter_context(tc.psum_pool(name="psum_h", bufs=4))
+        psum_acc = ctx.enter_context(tc.psum_pool(name="psum_acc", bufs=1))
+
+        raw_of = {}
+        grouped_of = {}
+        codes_of = {}
+        h_of = {}
+        bn = {}
+
+        def load_slab(s):
+            if s >= SLABS:
+                return
+            raw = raw_pool.tile([P, PACK, DO], BF16, name="raw")
+            if s < W_SLABS:
+                rows = W[s // W_PASSES, (s % W_PASSES) * K_PASS : (s % W_PASSES + 1) * K_PASS, :]
+                nc.sync.dma_start(out=raw[:], in_=rows.rearrange("(p t) w -> p t w", t=PACK))
+            else:
+                g = s - W_SLABS
+                rows = Wf1[g * K_PASS : (g + 1) * K_PASS, :].rearrange("(q t i) w -> t q i w", t=PACK, i=RUN)
+                for t in range(PACK):
+                    nc.sync.dma_start(out=raw[:, t, :], in_=rows[t])
+            raw_of[s] = raw
+
+        def regroup_slab(s, vector_cols):
+            if s >= SLABS:
+                return
+            grouped = slab_pool.tile([P, DO, PACK], BF16, name="grouped", align_bytes=64)
+            if s < W_SLABS:
+                src = raw_of[s].rearrange("p k (q t i) -> p q t k i", t=PACK, i=RUN)
+                dst = grouped.rearrange("p (t q i) k -> p q t k i", t=PACK, i=RUN)
+                cut = vector_cols // (PACK * RUN)
+            else:
+                src = raw_of[s].rearrange("p k (c i) -> p c k i", i=RUN)
+                dst = grouped.rearrange("p (c i) k -> p c k i", i=RUN)
+                cut = vector_cols // RUN
+            nc.vector.tensor_copy(out=dst[:, :cut], in_=src[:, :cut])
+            nc.scalar.copy(out=dst[:, cut:], in_=src[:, cut:])
+            grouped_of[s] = grouped
+
+        def quantise_slab(s):
+            if s < 0:
+                return
+            codes = slab_pool.tile([P, DO], U32, name="codes", align_bytes=64)
+            scales = slab_pool.tile([P, DO], U8, name="scales", align_bytes=64)
+            nc.vector.quantize_mx(
+                out=codes[:].bitcast(FP8X4),
+                scales=scales[:],
+                in_=grouped_of[s].rearrange("p w t -> p (w t)"),
+            )
+            codes_of[s] = (codes, scales)
+
+        def stage1(br):
+            h_of[br] = []
+            for pair in range(TILES // 2):
+                h = psum_h.tile([P, 2, B], F32, name="h")
+                for half in range(2):
+                    j, t = divmod(2 * pair + half, PACK)
+                    cols = slice((GROUPS * t + j) * P, (GROUPS * t + j + 1) * P)
+                    for c in range(W_PASSES):
+                        codes, scales = codes_of[W_PASSES * br + c]
+                        nc.tensor.matmul_mx(
+                            out=h[:, half, :],
+                            lhsT=codes[:, cols].bitcast(FP8X4),
+                            lhsT_scale=scales[:, cols],
+                            rhs=x_codes[:, c * B : (c + 1) * B].bitcast(FP8X4),
+                            rhs_scale=x_scales[:, c * B : (c + 1) * B],
+                            start=(c == 0),
+                            stop=(c == W_PASSES - 1),
+                        )
+                h_of[br].append(h)
+
+        def stage2(g):
+            codes, scales = codes_of[W_SLABS + g]
+            for bt in range(B // P):
+                rows = slice(bt * P, (bt + 1) * P)
+                for nt in range(DO // N_TILE):
+                    cols = slice(nt * N_TILE, (nt + 1) * N_TILE)
+                    nc.tensor.matmul_mx(
+                        out=acc[bt][nt][:],
+                        lhsT=f_codes[:, g, rows].bitcast(FP8X4),
+                        lhsT_scale=f_scales[:, g, rows],
+                        rhs=codes[:, cols].bitcast(FP8X4),
+                        rhs_scale=scales[:, cols],
+                        start=(g == 0),
+                        stop=(g == F // K_PASS - 1),
+                    )
+
+        def live(br):
+            return 0 <= br < NB
+
+        def stat_tile(name, br):
+            bn[(name, br)] = branch_pool.tile([P, TILES], F32, name=name)
+            return bn[(name, br)]
+
+        def relu_and_sums(br):
+            if not live(br):
+                return
+            a = branch_pool.tile([P, TILES, B], F32, name="a")
+            bn[("a", br)] = a
+            sums = stat_tile("sums", br)
+            for i in range(TILES):
+                nc.scalar.activation(
+                    out=a[:, i, :],
+                    in_=h_of[br][i // 2][:, i % 2, :],
+                    func=ACT.Relu,
+                    bias=params[:, i, br : br + 1],
+                    accum_out=sums[:, i : i + 1],
+                )
+
+        def negative_mean(br):
+            if live(br):
+                nc.scalar.mul(out=stat_tile("neg_mean", br)[:], in_=bn[("sums", br)][:], mul=-1.0 / B)
+
+        def squares(br):
+            if not live(br):
+                return
+            unused = branch_pool.tile([P, TILES, B], BF16, name="unused")
+            sumsq = stat_tile("sumsq", br)
+            for i in range(TILES):
+                nc.scalar.activation(
+                    out=unused[:, i, :],
+                    in_=bn[("a", br)][:, i, :],
+                    func=ACT.Square,
+                    bias=bn[("neg_mean", br)][:, i : i + 1],
+                    accum_out=sumsq[:, i : i + 1],
+                )
+
+        def standard_deviation(br):
+            if live(br):
+                nc.scalar.activation(
+                    out=stat_tile("std", br)[:], in_=bn[("sumsq", br)][:], func=ACT.Sqrt, bias=eps_col[:], scale=1.0 / B
+                )
+
+        def reciprocal_std(br):
+            if live(br):
+                nc.vector.reciprocal(out=stat_tile("rstd", br)[:], in_=bn[("std", br)][:])
+
+        def gain(br):
+            if live(br):
+                nc.vector.tensor_mul(
+                    out=stat_tile("gain", br)[:], in0=bn[("rstd", br)][:], in1=params[:, :, NB + br]
+                )
+
+        def negative_mean_times_gain(br):
+            if live(br):
+                nc.vector.tensor_mul(out=stat_tile("moved", br)[:], in0=bn[("neg_mean", br)][:], in1=bn[("gain", br)][:])
+
+        def shift(br):
+            if live(br):
+                nc.vector.tensor_add(
+                    out=stat_tile("shift", br)[:], in0=bn[("moved", br)][:], in1=params[:, :, 2 * NB + br]
+                )
+
+        def normalise(br):
+            if not live(br):
+                return
+            normed = branch_pool.tile([P, TILES, B], BF16, name="normed")
+            bn[("normed", br)] = normed
+            for i in range(TILES):
+                nc.vector.tensor_scalar(
+                    out=normed[:, i, :],
+                    in0=bn[("a", br)][:, i, :],
+                    scalar1=bn[("gain", br)][:, i : i + 1],
+                    scalar2=bn[("shift", br)][:, i : i + 1],
+                    op0=ALU.mult,
+                    op1=ALU.add,
+                )
+
+        def regroup_fused(br, j):
+            if not live(br):
+                return
+            if j == 0:
+                bn[("f_grouped", br)] = branch_pool.tile([P, GROUPS, B, PACK], BF16, name="f_grouped", align_bytes=64)
+            nc.vector.tensor_copy(
+                out=bn[("f_grouped", br)][:, j].rearrange("p (c i) t -> p c t i", i=RUN),
+                in_=bn[("normed", br)][:, PACK * j : PACK * (j + 1), :].rearrange("p t (c i) -> p c t i", i=RUN),
+            )
+
+        def quantise_fused(br):
+            if live(br):
+                passes = slice(GROUPS * br, GROUPS * (br + 1))
+                nc.vector.quantize_mx(
+                    out=f_codes[:, passes, :].rearrange("p g n -> p (g n)").bitcast(FP8X4),
+                    scales=f_scales[:, passes, :].rearrange("p g n -> p (g n)"),
+                    in_=bn[("f_grouped", br)].rearrange("p g n t -> p (g n t)"),
+                )
+
+        x_sb = const.tile([P, (B // P) * DI], BF16, name="x_sb")
+        for s in range(ROUND_SLABS):
+            load_slab(s)
+        nc.sync.dma_start(
+            out=x_sb.rearrange("p (bt k) -> p bt k", k=DI), in_=x.rearrange("(bt p) k -> p bt k", p=P)
+        )
+        for s in range(ROUND_SLABS, RAW_BUFS):
+            load_slab(s)
+        bias_all = const.tile([P, DO], BF16, name="bias_all")
+        nc.sync.dma_start(out=bias_all[:], in_=bf1.partition_broadcast(P))
+
+        param_rows = 3 * NB
+        rows = const.tile([P, DO], BF16, name="rows")
+        nc.vector.memset(rows[:], 0.0)
+        eps_col = const.tile([P, 1], F32, name="eps_col")
+        nc.vector.memset(eps_col[:], EPS)
+        for i, vectors in enumerate((b, gamma, beta)):
+            nc.scalar.dma_start(out=rows[NB * i : NB * (i + 1), :], in_=vectors)
+        first_sqrt = const.tile([P, 1], F32, name="first_sqrt")
+        nc.scalar.activation(out=first_sqrt[:], in_=eps_col[:], func=ACT.Sqrt)
+
+        ident_f32 = const.tile([P, P], F32, name="ident_f32")
+        make_identity(nc, ident_f32[:])
+        ident_bf16 = const.tile([P, P], BF16, name="ident_bf16")
+        make_identity(nc, ident_bf16[:])
+
+        x_grouped = const.tile([P, W_PASSES * B * PACK], BF16, name="x_grouped", align_bytes=64)
+        x_codes = const.tile([P, W_PASSES * B], U32, name="x_codes", align_bytes=64)
+        x_scales = const.tile([P, W_PASSES * B], U8, name="x_scales", align_bytes=64)
+        rows_by_tile = const.tile([P, DO], BF16, name="rows_by_tile")
+        params = const.tile([P, TILES, param_rows], F32, name="params")
+        f_codes = const.tile([P, F // K_PASS, B], U32, name="f_codes", align_bytes=64)
+        f_scales = const.tile([P, F // K_PASS, B], U8, name="f_scales", align_bytes=64)
+        acc = [
+            [psum_acc.tile([P, N_TILE], F32, name="acc%d%d" % (bt, nt)) for nt in range(DO // N_TILE)]
+            for bt in range(B // P)
+        ]
+
+        def prepare_x_and_params():
+            x_words = x_sb[:].bitcast(F32).rearrange("p (bt c q u) -> p bt c q u", bt=B // P, c=W_PASSES, q=P)
+            x_grouped_words = x_grouped[:].bitcast(F32).rearrange("p (c n u) -> p c n u", c=W_PASSES, n=B)
+            x_t = []
+            for c in range(W_PASSES):
+                x_t.append(psum_h.tile([P, 2, B], F32, name="h"))
+                for u in range(2):
+                    for bt in range(B // P):
+                        nc.tensor.transpose(x_t[c][:, u, bt * P : (bt + 1) * P], x_words[:, bt, c, :, u], ident_f32[:])
+            nc.vector.tensor_copy(
+                out=rows_by_tile.rearrange("p (j t q i) -> p j q t i", j=GROUPS, t=PACK, i=RUN),
+                in_=rows.rearrange("p (j q t i) -> p j q t i", j=GROUPS, t=PACK, i=RUN),
+            )
+            params_t = psum_h.tile([P, TILES, P], BF16, name="h")
+            for i in range(TILES):
+                nc.tensor.transpose(params_t[:, i, :], rows_by_tile[:, i * P : (i + 1) * P], ident_bf16[:])
+            nc.vector.tensor_copy(out=x_grouped_words[:, 0], in_=x_t[0].rearrange("p u n -> p n u"))
+            nc.scalar.copy(out=x_grouped_words[:, 1], in_=x_t[1].rearrange("p u n -> p n u"))
+            nc.vector.tensor_copy(out=params[:], in_=params_t[:, :, :param_rows])
+            nc.vector.quantize_mx(out=x_codes[:].bitcast(FP8X4), scales=x_scales[:], in_=x_grouped[:])
+
+        def run_round(r):
+            first = ROUND_SLABS * r
+            vector_cols = BASE_COLS
+            if live(r - 2):
+                vector_cols += RELU_SQUARES_COLS
+            if live(r - 3):
+                vector_cols -= NORMALISE_COLS
+            if live(r - 4):
+                vector_cols -= FUSED_COLS
+
+            relu_and_sums(r - 2)
+            standard_deviation(r - 3)
+            quantise_slab(first - 2)
+            quantise_slab(first - 1)
+            if 1 <= r <= NB:
+                stage1(r - 1)
+            if r > NB:
+                stage2(first - 2 - W_SLABS)
+                stage2(first - 1 - W_SLABS)
+
+            regroup_slab(first, vector_cols)
+            reciprocal_std(r - 3)
+            negative_mean(r - 2)
+            regroup_slab(first + 1, vector_cols)
+            load_slab(first + RAW_BUFS)
+            load_slab(first + RAW_BUFS + 1)
+            squares(r - 2)
+
+            gain(r - 3)
+            regroup_fused(r - 4, 0)
+            negative_mean_times_gain(r - 3)
+            regroup_fused(r - 4, 1)
+            shift(r - 3)
+            normalise(r - 3)
+            quantise_fused(r - 4)
+
+        run_round(0)
+        prepare_x_and_params()
+        for r in range(1, ROUNDS + 1):
+            run_round(r)
+
+        for bt in range(B // P):
+            for nt in range(DO // N_TILE):
+                cols = slice(nt * N_TILE, (nt + 1) * N_TILE)
+                result = result_pool.tile([P, N_TILE], F32, name="result")
+                nc.vector.tensor_tensor(out=result[:], in0=acc[bt][nt][:], in1=bias_all[:, cols], op=ALU.add)
+                nc.scalar.activation(out=result[:], in_=result[:], func=ACT.Relu)
+                nc.sync.dma_start(out=out[bt * P : (bt + 1) * P, cols], in_=result[:])

@@ -34,6 +34,8 @@ BASE_COLS = 448
 RELU_SQUARES_COLS = 480
 NORMALISE_COLS = 128
 FUSED_COLS = 128
+HEAD_PIECES = 4
+LAST_COLS = 128
 
 
 def tile_extremeoptimizationlayer_pa_kernel(tc, x, W, b, gamma, beta, Wf1, bf1, out):
@@ -53,13 +55,16 @@ def tile_extremeoptimizationlayer_pa_kernel(tc, x, W, b, gamma, beta, Wf1, bf1, 
         h_of = {}
         bn = {}
 
-        def load_slab(s):
+        def load_slab(s, pieces=1):
             if s >= SLABS:
                 return
             raw = raw_pool.tile([P, PACK, DO], BF16, name="raw")
             if s < W_SLABS:
                 rows = W[s // W_PASSES, (s % W_PASSES) * K_PASS : (s % W_PASSES + 1) * K_PASS, :]
-                nc.sync.dma_start(out=raw[:], in_=rows.rearrange("(p t) w -> p t w", t=PACK))
+                width = DO // pieces
+                for i in range(pieces):
+                    cols = slice(i * width, (i + 1) * width)
+                    nc.sync.dma_start(out=raw[:, :, cols], in_=rows[:, cols].rearrange("(p t) w -> p t w", t=PACK))
             else:
                 g = s - W_SLABS
                 rows = Wf1[g * K_PASS : (g + 1) * K_PASS, :].rearrange("(q t i) w -> t q i w", t=PACK, i=RUN)
@@ -67,33 +72,36 @@ def tile_extremeoptimizationlayer_pa_kernel(tc, x, W, b, gamma, beta, Wf1, bf1, 
                     nc.sync.dma_start(out=raw[:, t, :], in_=rows[t])
             raw_of[s] = raw
 
-        def regroup_slab(s, vector_cols):
-            if s >= SLABS:
-                return
-            grouped = slab_pool.tile([P, DO, PACK], BF16, name="grouped", align_bytes=64)
+        def regroup(engine_copy, s, first, last):
+            if s not in grouped_of:
+                grouped = slab_pool.tile([P, DO, PACK], BF16, name="grouped", align_bytes=64)
+                grouped_of[s] = grouped
+            grouped = grouped_of[s]
             if s < W_SLABS:
                 src = raw_of[s].rearrange("p k (q t i) -> p q t k i", t=PACK, i=RUN)
                 dst = grouped.rearrange("p (t q i) k -> p q t k i", t=PACK, i=RUN)
-                cut = vector_cols // (PACK * RUN)
+                runs = slice(first // (PACK * RUN), last // (PACK * RUN))
             else:
                 src = raw_of[s].rearrange("p k (c i) -> p c k i", i=RUN)
                 dst = grouped.rearrange("p (c i) k -> p c k i", i=RUN)
-                cut = vector_cols // RUN
-            nc.vector.tensor_copy(out=dst[:, :cut], in_=src[:, :cut])
-            nc.scalar.copy(out=dst[:, cut:], in_=src[:, cut:])
-            grouped_of[s] = grouped
+                runs = slice(first // RUN, last // RUN)
+            engine_copy(out=dst[:, runs], in_=src[:, runs])
 
-        def quantise_slab(s):
-            if s < 0:
-                return
-            codes = slab_pool.tile([P, DO], U32, name="codes", align_bytes=64)
-            scales = slab_pool.tile([P, DO], U8, name="scales", align_bytes=64)
+        def regroup_slab(s, vector_cols):
+            regroup(nc.vector.tensor_copy, s, 0, vector_cols)
+            regroup(nc.scalar.copy, s, vector_cols, DO)
+
+        def quantise_slab(s, first=0, last=DO):
+            if s not in codes_of:
+                codes = slab_pool.tile([P, DO], U32, name="codes", align_bytes=64)
+                scales = slab_pool.tile([P, DO], U8, name="scales", align_bytes=64)
+                codes_of[s] = (codes, scales)
+            codes, scales = codes_of[s]
             nc.vector.quantize_mx(
-                out=codes[:].bitcast(FP8X4),
-                scales=scales[:],
-                in_=grouped_of[s].rearrange("p w t -> p (w t)"),
+                out=codes[:, first:last].bitcast(FP8X4),
+                scales=scales[:, first:last],
+                in_=grouped_of[s][:, first:last, :].rearrange("p w t -> p (w t)"),
             )
-            codes_of[s] = (codes, scales)
 
         def stage1(br):
             h_of[br] = []
@@ -115,11 +123,11 @@ def tile_extremeoptimizationlayer_pa_kernel(tc, x, W, b, gamma, beta, Wf1, bf1, 
                         )
                 h_of[br].append(h)
 
-        def stage2(g):
+        def stage2(g, column_tiles=range(DO // N_TILE)):
             codes, scales = codes_of[W_SLABS + g]
             for bt in range(B // P):
                 rows = slice(bt * P, (bt + 1) * P)
-                for nt in range(DO // N_TILE):
+                for nt in column_tiles:
                     cols = slice(nt * N_TILE, (nt + 1) * N_TILE)
                     nc.tensor.matmul_mx(
                         out=acc[bt][nt][:],
@@ -233,7 +241,7 @@ def tile_extremeoptimizationlayer_pa_kernel(tc, x, W, b, gamma, beta, Wf1, bf1, 
 
         x_sb = const.tile([P, (B // P) * DI], BF16, name="x_sb")
         for s in range(ROUND_SLABS):
-            load_slab(s)
+            load_slab(s, pieces=HEAD_PIECES)
         nc.sync.dma_start(
             out=x_sb.rearrange("p (bt k) -> p bt k", k=DI), in_=x.rearrange("(bt p) k -> p bt k", p=P)
         )
@@ -243,12 +251,11 @@ def tile_extremeoptimizationlayer_pa_kernel(tc, x, W, b, gamma, beta, Wf1, bf1, 
         nc.sync.dma_start(out=bias_all[:], in_=bf1.partition_broadcast(P))
 
         param_rows = 3 * NB
-        rows = const.tile([P, DO], BF16, name="rows")
-        nc.vector.memset(rows[:], 0.0)
+        rows = const.tile([32, DO], BF16, name="rows")
+        for i, vectors in enumerate((b, gamma, beta, b)):
+            nc.scalar.dma_start(out=rows[NB * i : NB * (i + 1), :], in_=vectors)
         eps_col = const.tile([P, 1], F32, name="eps_col")
         nc.vector.memset(eps_col[:], EPS)
-        for i, vectors in enumerate((b, gamma, beta)):
-            nc.scalar.dma_start(out=rows[NB * i : NB * (i + 1), :], in_=vectors)
         first_sqrt = const.tile([P, 1], F32, name="first_sqrt")
         nc.scalar.activation(out=first_sqrt[:], in_=eps_col[:], func=ACT.Sqrt)
 
@@ -261,6 +268,18 @@ def tile_extremeoptimizationlayer_pa_kernel(tc, x, W, b, gamma, beta, Wf1, bf1, 
         x_codes = const.tile([P, W_PASSES * B], U32, name="x_codes", align_bytes=64)
         x_scales = const.tile([P, W_PASSES * B], U8, name="x_scales", align_bytes=64)
         rows_by_tile = const.tile([P, DO], BF16, name="rows_by_tile")
+        nc.gpsimd.memset(rows_by_tile[32:64, :], 0.0)
+        nc.gpsimd.memset(rows_by_tile[64:128, :], 0.0)
+        for j in range(GROUPS):
+            features = slice(j * K_PASS, (j + 1) * K_PASS)
+            nc.gpsimd.tensor_scalar(
+                out=rows_by_tile[:32, features].rearrange("p (t q i) -> p q t i", t=PACK, i=RUN),
+                in0=rows[:, features].rearrange("p (q t i) -> p q t i", t=PACK, i=RUN),
+                scalar1=1.0,
+                scalar2=0.0,
+                op0=ALU.mult,
+                op1=ALU.add,
+            )
         params = const.tile([P, TILES, param_rows], F32, name="params")
         f_codes = const.tile([P, F // K_PASS, B], U32, name="f_codes", align_bytes=64)
         f_scales = const.tile([P, F // K_PASS, B], U8, name="f_scales", align_bytes=64)
@@ -269,7 +288,7 @@ def tile_extremeoptimizationlayer_pa_kernel(tc, x, W, b, gamma, beta, Wf1, bf1, 
             for bt in range(B // P)
         ]
 
-        def prepare_x_and_params():
+        def prepare_x():
             x_words = x_sb[:].bitcast(F32).rearrange("p (bt c q u) -> p bt c q u", bt=B // P, c=W_PASSES, q=P)
             x_grouped_words = x_grouped[:].bitcast(F32).rearrange("p (c n u) -> p c n u", c=W_PASSES, n=B)
             x_t = []
@@ -278,17 +297,25 @@ def tile_extremeoptimizationlayer_pa_kernel(tc, x, W, b, gamma, beta, Wf1, bf1, 
                 for u in range(2):
                     for bt in range(B // P):
                         nc.tensor.transpose(x_t[c][:, u, bt * P : (bt + 1) * P], x_words[:, bt, c, :, u], ident_f32[:])
-            nc.vector.tensor_copy(
-                out=rows_by_tile.rearrange("p (j t q i) -> p j q t i", j=GROUPS, t=PACK, i=RUN),
-                in_=rows.rearrange("p (j q t i) -> p j q t i", j=GROUPS, t=PACK, i=RUN),
-            )
-            params_t = psum_h.tile([P, TILES, P], BF16, name="h")
-            for i in range(TILES):
-                nc.tensor.transpose(params_t[:, i, :], rows_by_tile[:, i * P : (i + 1) * P], ident_bf16[:])
             nc.vector.tensor_copy(out=x_grouped_words[:, 0], in_=x_t[0].rearrange("p u n -> p n u"))
             nc.scalar.copy(out=x_grouped_words[:, 1], in_=x_t[1].rearrange("p u n -> p n u"))
-            nc.vector.tensor_copy(out=params[:], in_=params_t[:, :, :param_rows])
             nc.vector.quantize_mx(out=x_codes[:].bitcast(FP8X4), scales=x_scales[:], in_=x_grouped[:])
+
+        def prepare_params():
+            params_t = acc[-1][-1][:].bitcast(BF16).rearrange("p (i n) -> p i n", i=TILES)
+            for i in range(TILES):
+                nc.tensor.transpose(params_t[:, i, :], rows_by_tile[:, i * P : (i + 1) * P], ident_bf16[:])
+            nc.vector.tensor_copy(out=params[:], in_=params_t[:, :, :param_rows])
+
+        def quantise_and_multiply(r):
+            slabs = range(ROUND_SLABS * r, ROUND_SLABS * (r + 1))
+            for s in slabs:
+                quantise_slab(s)
+            if r < NB:
+                stage1(r)
+            else:
+                for s in slabs:
+                    stage2(s - W_SLABS)
 
         def run_round(r):
             first = ROUND_SLABS * r
@@ -302,13 +329,7 @@ def tile_extremeoptimizationlayer_pa_kernel(tc, x, W, b, gamma, beta, Wf1, bf1, 
 
             relu_and_sums(r - 2)
             standard_deviation(r - 3)
-            quantise_slab(first - 2)
-            quantise_slab(first - 1)
-            if 1 <= r <= NB:
-                stage1(r - 1)
-            if r > NB:
-                stage2(first - 2 - W_SLABS)
-                stage2(first - 1 - W_SLABS)
+            quantise_and_multiply(r - 1)
 
             regroup_slab(first, vector_cols)
             reciprocal_std(r - 3)
@@ -326,15 +347,40 @@ def tile_extremeoptimizationlayer_pa_kernel(tc, x, W, b, gamma, beta, Wf1, bf1, 
             normalise(r - 3)
             quantise_fused(r - 4)
 
-        run_round(0)
-        prepare_x_and_params()
-        for r in range(1, ROUNDS + 1):
-            run_round(r)
-
-        for bt in range(B // P):
-            for nt in range(DO // N_TILE):
-                cols = slice(nt * N_TILE, (nt + 1) * N_TILE)
+        def store(nt):
+            cols = slice(nt * N_TILE, (nt + 1) * N_TILE)
+            for bt in range(B // P):
                 result = result_pool.tile([P, N_TILE], F32, name="result")
                 nc.vector.tensor_tensor(out=result[:], in0=acc[bt][nt][:], in1=bias_all[:, cols], op=ALU.add)
                 nc.scalar.activation(out=result[:], in_=result[:], func=ACT.Relu)
                 nc.sync.dma_start(out=out[bt * P : (bt + 1) * P, cols], in_=result[:])
+
+        def first_round():
+            piece = DO // HEAD_PIECES
+            for s, scalar_pieces in ((0, (1,)), (1, (0, 1))):
+                for i in range(HEAD_PIECES):
+                    copy = nc.scalar.copy if i in scalar_pieces else nc.vector.tensor_copy
+                    regroup(copy, s, i * piece, (i + 1) * piece)
+                load_slab(s + RAW_BUFS)
+
+        def last_round():
+            quantise_and_multiply(ROUNDS - 2)
+            slabs = range(SLABS - ROUND_SLABS, SLABS)
+            halves = [(nt * N_TILE, (nt + 1) * N_TILE) for nt in range(DO // N_TILE)]
+            for first, last in halves:
+                for s in slabs:
+                    regroup(nc.vector.tensor_copy, s, first, first + LAST_COLS)
+                    regroup(nc.scalar.copy, s, first + LAST_COLS, last)
+            for nt, (first, last) in enumerate(halves):
+                for s in slabs:
+                    quantise_slab(s, first, last)
+                    stage2(s - W_SLABS, (nt,))
+                store(nt)
+
+        first_round()
+        prepare_x()
+        run_round(1)
+        prepare_params()
+        for r in range(2, ROUNDS - 1):
+            run_round(r)
+        last_round()

@@ -34,6 +34,10 @@ BASE_COLS = 448
 RELU_SQUARES_COLS = 480
 NORMALISE_COLS = 128
 FUSED_COLS = 128
+TENSOR_COLS = 256
+TENSOR_SLABS = range(2, 27)
+TENSOR_SLABS_IN_ACC = 18
+TENSOR_SHIFT_COLS = 64
 HEAD_PIECES = 4
 LAST_COLS = 128
 
@@ -52,6 +56,7 @@ def tile_extremeoptimizationlayer_pa_kernel(tc, x, W, b, gamma, beta, Wf1, bf1, 
         raw_of = {}
         grouped_of = {}
         codes_of = {}
+        bank_of = {}
         h_of = {}
         bn = {}
 
@@ -87,9 +92,45 @@ def tile_extremeoptimizationlayer_pa_kernel(tc, x, W, b, gamma, beta, Wf1, bf1, 
                 runs = slice(first // RUN, last // RUN)
             engine_copy(out=dst[:, runs], in_=src[:, runs])
 
+        def interleave_on_tensor(s):
+            if s not in TENSOR_SLABS:
+                return
+            if s < TENSOR_SLABS_IN_ACC:
+                bank = acc[s % 2][s // 2 % 2][:].bitcast(BF16).rearrange("p (c k) -> p c k", k=PACK)
+            else:
+                bank = psum_h.tile([P, TENSOR_COLS, PACK], BF16, name="h")
+            bank_of[s] = bank
+            cols = N_TILE // PACK
+            for first in range(0, TENSOR_COLS, cols):
+                nc.tensor.matmul(
+                    out=bank[:, first : first + cols, :].rearrange("p c k -> p k c"),
+                    lhsT=ident_bf16[:],
+                    rhs=raw_of[s][:, :, DO - TENSOR_COLS + first : DO - TENSOR_COLS + first + cols],
+                    start=True,
+                    stop=True,
+                )
+
+        def copy_from_tensor(s):
+            first = DO - TENSOR_COLS
+            if s < W_SLABS:
+                src = bank_of[s].rearrange("p (q t i) k -> p q t (i k)", t=PACK, i=RUN)
+                dst = grouped_of[s].rearrange("p (t q i) k -> p q t (i k)", t=PACK, i=RUN)[:, first // (PACK * RUN) :]
+            else:
+                src = bank_of[s]
+                dst = grouped_of[s][:, first:, :]
+            nc.scalar.copy(out=dst, in_=src)
+
         def regroup_slab(s, vector_cols):
+            if s not in TENSOR_SLABS:
+                regroup(nc.vector.tensor_copy, s, 0, vector_cols)
+                regroup(nc.scalar.copy, s, vector_cols, DO)
+                return
+            last = DO - TENSOR_COLS
+            vector_cols = min(vector_cols - TENSOR_SHIFT_COLS, last)
             regroup(nc.vector.tensor_copy, s, 0, vector_cols)
-            regroup(nc.scalar.copy, s, vector_cols, DO)
+            if vector_cols < last:
+                regroup(nc.scalar.copy, s, vector_cols, last)
+            copy_from_tensor(s)
 
         def quantise_slab(s, first=0, last=DO):
             if s not in codes_of:
@@ -346,6 +387,8 @@ def tile_extremeoptimizationlayer_pa_kernel(tc, x, W, b, gamma, beta, Wf1, bf1, 
             shift(r - 3)
             normalise(r - 3)
             quantise_fused(r - 4)
+            interleave_on_tensor(first + 2)
+            interleave_on_tensor(first + 3)
 
         def store(nt):
             cols = slice(nt * N_TILE, (nt + 1) * N_TILE)
@@ -379,6 +422,8 @@ def tile_extremeoptimizationlayer_pa_kernel(tc, x, W, b, gamma, beta, Wf1, bf1, 
 
         first_round()
         prepare_x()
+        interleave_on_tensor(2)
+        interleave_on_tensor(3)
         run_round(1)
         prepare_params()
         for r in range(2, ROUNDS - 1):

@@ -29,16 +29,18 @@ ROUNDS = SLABS // ROUND_SLABS
 N_TILE = 512
 RUN = 4
 
-RAW_BUFS = 10
+RAW_BUFS = 9
 BASE_COLS = 448
-RELU_SQUARES_COLS = 480
+RELU_COLS = 192
+SQUARES_COLS = 192
 NORMALISE_COLS = 128
 FUSED_COLS = 128
 TENSOR_COLS = 256
 TENSOR_SLABS = range(2, 27)
-TENSOR_SLABS_IN_ACC = 18
-TENSOR_SHIFT_COLS = 64
+TENSOR_SLABS_IN_ACC = 20
+ALONE_COLS = 64
 HEAD_PIECES = 4
+HEAD_COLS = DO // HEAD_PIECES
 LAST_COLS = 128
 
 
@@ -49,27 +51,38 @@ def tile_extremeoptimizationlayer_pa_kernel(tc, x, W, b, gamma, beta, Wf1, bf1, 
         raw_pool = ctx.enter_context(tc.tile_pool(name="raw", bufs=RAW_BUFS))
         slab_pool = ctx.enter_context(tc.tile_pool(name="slab", bufs=2 * ROUND_SLABS))
         branch_pool = ctx.enter_context(tc.tile_pool(name="branch", bufs=2))
+        stat_pool = ctx.enter_context(tc.tile_pool(name="stat", bufs=4))
+        a_pool = ctx.enter_context(tc.tile_pool(name="a", bufs=3))
+        unused_pool = ctx.enter_context(tc.tile_pool(name="unused", bufs=1))
         result_pool = ctx.enter_context(tc.tile_pool(name="result", bufs=4))
         psum_h = ctx.enter_context(tc.psum_pool(name="psum_h", bufs=4))
         psum_acc = ctx.enter_context(tc.psum_pool(name="psum_acc", bufs=1))
 
         raw_of = {}
+        pieces_of = {}
         grouped_of = {}
         codes_of = {}
         bank_of = {}
         h_of = {}
         bn = {}
 
-        def load_slab(s, pieces=1):
+        def rows_of_w(s):
+            return W[s // W_PASSES, (s % W_PASSES) * K_PASS : (s % W_PASSES + 1) * K_PASS, :]
+
+        def load_head_slab(s):
+            pieces_of[s] = []
+            for i in range(HEAD_PIECES):
+                piece = const.tile([P, PACK, HEAD_COLS], BF16, name="piece%d_%d" % (s, i))
+                cols = slice(i * HEAD_COLS, (i + 1) * HEAD_COLS)
+                nc.sync.dma_start(out=piece[:], in_=rows_of_w(s)[:, cols].rearrange("(p t) w -> p t w", t=PACK))
+                pieces_of[s].append(piece)
+
+        def load_slab(s):
             if s >= SLABS:
                 return
             raw = raw_pool.tile([P, PACK, DO], BF16, name="raw")
             if s < W_SLABS:
-                rows = W[s // W_PASSES, (s % W_PASSES) * K_PASS : (s % W_PASSES + 1) * K_PASS, :]
-                width = DO // pieces
-                for i in range(pieces):
-                    cols = slice(i * width, (i + 1) * width)
-                    nc.sync.dma_start(out=raw[:, :, cols], in_=rows[:, cols].rearrange("(p t) w -> p t w", t=PACK))
+                nc.sync.dma_start(out=raw[:], in_=rows_of_w(s).rearrange("(p t) w -> p t w", t=PACK))
             else:
                 g = s - W_SLABS
                 rows = Wf1[g * K_PASS : (g + 1) * K_PASS, :].rearrange("(q t i) w -> t q i w", t=PACK, i=RUN)
@@ -82,15 +95,18 @@ def tile_extremeoptimizationlayer_pa_kernel(tc, x, W, b, gamma, beta, Wf1, bf1, 
                 grouped = slab_pool.tile([P, DO, PACK], BF16, name="grouped", align_bytes=64)
                 grouped_of[s] = grouped
             grouped = grouped_of[s]
-            if s < W_SLABS:
-                src = raw_of[s].rearrange("p k (q t i) -> p q t k i", t=PACK, i=RUN)
-                dst = grouped.rearrange("p (t q i) k -> p q t k i", t=PACK, i=RUN)
-                runs = slice(first // (PACK * RUN), last // (PACK * RUN))
+            if s in pieces_of:
+                src = pieces_of[s][first // HEAD_COLS]
             else:
-                src = raw_of[s].rearrange("p k (c i) -> p c k i", i=RUN)
-                dst = grouped.rearrange("p (c i) k -> p c k i", i=RUN)
-                runs = slice(first // RUN, last // RUN)
-            engine_copy(out=dst[:, runs], in_=src[:, runs])
+                src = raw_of[s][:, :, first:last]
+            if s < W_SLABS:
+                src = src.rearrange("p k (q t i) -> p q t k i", t=PACK, i=RUN)
+                dst = grouped.rearrange("p (t q i) k -> p q t k i", t=PACK, i=RUN)
+                dst = dst[:, first // (PACK * RUN) : last // (PACK * RUN)]
+            else:
+                src = src.rearrange("p k (c i) -> p c k i", i=RUN)
+                dst = grouped[:, first:last, :].rearrange("p (c i) k -> p c k i", i=RUN)
+            engine_copy(out=dst, in_=src)
 
         def interleave_on_tensor(s):
             if s not in TENSOR_SLABS:
@@ -116,17 +132,18 @@ def tile_extremeoptimizationlayer_pa_kernel(tc, x, W, b, gamma, beta, Wf1, bf1, 
                 src = bank_of[s].rearrange("p (q t i) k -> p q t (i k)", t=PACK, i=RUN)
                 dst = grouped_of[s].rearrange("p (t q i) k -> p q t (i k)", t=PACK, i=RUN)[:, first // (PACK * RUN) :]
             else:
-                src = bank_of[s]
-                dst = grouped_of[s][:, first:, :]
-            nc.scalar.copy(out=dst, in_=src)
+                src = bank_of[s].rearrange("p c k -> p (c k)")
+                dst = grouped_of[s][:, first:, :].rearrange("p c k -> p (c k)")
+            nc.scalar.copy(out=dst.bitcast(F32), in_=src.bitcast(F32))
 
         def regroup_slab(s, vector_cols):
             if s not in TENSOR_SLABS:
+                vector_cols += ALONE_COLS
                 regroup(nc.vector.tensor_copy, s, 0, vector_cols)
                 regroup(nc.scalar.copy, s, vector_cols, DO)
                 return
             last = DO - TENSOR_COLS
-            vector_cols = min(vector_cols - TENSOR_SHIFT_COLS, last)
+            vector_cols = min(vector_cols, last)
             regroup(nc.vector.tensor_copy, s, 0, vector_cols)
             if vector_cols < last:
                 regroup(nc.scalar.copy, s, vector_cols, last)
@@ -184,13 +201,20 @@ def tile_extremeoptimizationlayer_pa_kernel(tc, x, W, b, gamma, beta, Wf1, bf1, 
             return 0 <= br < NB
 
         def stat_tile(name, br):
-            bn[(name, br)] = branch_pool.tile([P, TILES], F32, name=name)
+            bn[(name, br)] = stat_pool.tile([P, TILES], F32, name=name)
             return bn[(name, br)]
+
+        def by_pass(stat):
+            return stat.rearrange("p (j t) -> p j t", t=PACK)
+
+        def branch_params(vector, br):
+            first = GROUPS * (NB * vector + br)
+            return params[:, :, first : first + GROUPS].rearrange("p t j -> p j t")
 
         def relu_and_sums(br):
             if not live(br):
                 return
-            a = branch_pool.tile([P, TILES, B], F32, name="a")
+            a = a_pool.tile([P, TILES, B], F32, name="a")
             bn[("a", br)] = a
             sums = stat_tile("sums", br)
             for i in range(TILES):
@@ -198,7 +222,7 @@ def tile_extremeoptimizationlayer_pa_kernel(tc, x, W, b, gamma, beta, Wf1, bf1, 
                     out=a[:, i, :],
                     in_=h_of[br][i // 2][:, i % 2, :],
                     func=ACT.Relu,
-                    bias=params[:, i, br : br + 1],
+                    bias=params[:, i % PACK, GROUPS * br + i // PACK : GROUPS * br + i // PACK + 1],
                     accum_out=sums[:, i : i + 1],
                 )
 
@@ -209,7 +233,7 @@ def tile_extremeoptimizationlayer_pa_kernel(tc, x, W, b, gamma, beta, Wf1, bf1, 
         def squares(br):
             if not live(br):
                 return
-            unused = branch_pool.tile([P, TILES, B], BF16, name="unused")
+            unused = unused_pool.tile([P, TILES, B], BF16, name="unused")
             sumsq = stat_tile("sumsq", br)
             for i in range(TILES):
                 nc.scalar.activation(
@@ -233,7 +257,7 @@ def tile_extremeoptimizationlayer_pa_kernel(tc, x, W, b, gamma, beta, Wf1, bf1, 
         def gain(br):
             if live(br):
                 nc.vector.tensor_mul(
-                    out=stat_tile("gain", br)[:], in0=bn[("rstd", br)][:], in1=params[:, :, NB + br]
+                    out=by_pass(stat_tile("gain", br)), in0=by_pass(bn[("rstd", br)]), in1=branch_params(1, br)
                 )
 
         def negative_mean_times_gain(br):
@@ -243,7 +267,7 @@ def tile_extremeoptimizationlayer_pa_kernel(tc, x, W, b, gamma, beta, Wf1, bf1, 
         def shift(br):
             if live(br):
                 nc.vector.tensor_add(
-                    out=stat_tile("shift", br)[:], in0=bn[("moved", br)][:], in1=params[:, :, 2 * NB + br]
+                    out=by_pass(stat_tile("shift", br)), in0=by_pass(bn[("moved", br)]), in1=branch_params(2, br)
                 )
 
         def normalise(br):
@@ -282,19 +306,21 @@ def tile_extremeoptimizationlayer_pa_kernel(tc, x, W, b, gamma, beta, Wf1, bf1, 
 
         x_sb = const.tile([P, (B // P) * DI], BF16, name="x_sb")
         for s in range(ROUND_SLABS):
-            load_slab(s, pieces=HEAD_PIECES)
+            load_head_slab(s)
         nc.sync.dma_start(
             out=x_sb.rearrange("p (bt k) -> p bt k", k=DI), in_=x.rearrange("(bt p) k -> p bt k", p=P)
         )
-        for s in range(ROUND_SLABS, RAW_BUFS):
+        for s in range(ROUND_SLABS, ROUND_SLABS + RAW_BUFS):
             load_slab(s)
         bias_all = const.tile([P, DO], BF16, name="bias_all")
         nc.sync.dma_start(out=bias_all[:], in_=bf1.partition_broadcast(P))
 
-        param_rows = 3 * NB
-        rows = const.tile([32, DO], BF16, name="rows")
-        for i, vectors in enumerate((b, gamma, beta, b)):
-            nc.scalar.dma_start(out=rows[NB * i : NB * (i + 1), :], in_=vectors)
+        vector_rows = GROUPS * NB
+        rows = const.tile([P // 2, K_PASS], BF16, name="rows")
+        for v, vectors in enumerate((b, gamma, beta, b)):
+            nc.scalar.dma_start(
+                out=rows[vector_rows * v : vector_rows * (v + 1), :], in_=vectors.rearrange("k (j f) -> (k j) f", j=GROUPS)
+            )
         eps_col = const.tile([P, 1], F32, name="eps_col")
         nc.vector.memset(eps_col[:], EPS)
         first_sqrt = const.tile([P, 1], F32, name="first_sqrt")
@@ -308,20 +334,17 @@ def tile_extremeoptimizationlayer_pa_kernel(tc, x, W, b, gamma, beta, Wf1, bf1, 
         x_grouped = const.tile([P, W_PASSES * B * PACK], BF16, name="x_grouped", align_bytes=64)
         x_codes = const.tile([P, W_PASSES * B], U32, name="x_codes", align_bytes=64)
         x_scales = const.tile([P, W_PASSES * B], U8, name="x_scales", align_bytes=64)
-        rows_by_tile = const.tile([P, DO], BF16, name="rows_by_tile")
-        nc.gpsimd.memset(rows_by_tile[32:64, :], 0.0)
-        nc.gpsimd.memset(rows_by_tile[64:128, :], 0.0)
-        for j in range(GROUPS):
-            features = slice(j * K_PASS, (j + 1) * K_PASS)
-            nc.gpsimd.tensor_scalar(
-                out=rows_by_tile[:32, features].rearrange("p (t q i) -> p q t i", t=PACK, i=RUN),
-                in0=rows[:, features].rearrange("p (q t i) -> p q t i", t=PACK, i=RUN),
-                scalar1=1.0,
-                scalar2=0.0,
-                op0=ALU.mult,
-                op1=ALU.add,
-            )
-        params = const.tile([P, TILES, param_rows], F32, name="params")
+        rows_by_tile = const.tile([P, PACK, P], BF16, name="rows_by_tile")
+        nc.gpsimd.memset(rows_by_tile[P // 2 :, :, :], 0.0)
+        nc.gpsimd.tensor_scalar(
+            out=rows_by_tile[: P // 2].rearrange("p t (q i) -> p q t i", i=RUN),
+            in0=rows.rearrange("p (q t i) -> p q t i", t=PACK, i=RUN),
+            scalar1=1.0,
+            scalar2=0.0,
+            op0=ALU.mult,
+            op1=ALU.add,
+        )
+        params = const.tile([P, PACK, 3 * vector_rows], F32, name="params")
         f_codes = const.tile([P, F // K_PASS, B], U32, name="f_codes", align_bytes=64)
         f_scales = const.tile([P, F // K_PASS, B], U8, name="f_scales", align_bytes=64)
         acc = [
@@ -343,52 +366,52 @@ def tile_extremeoptimizationlayer_pa_kernel(tc, x, W, b, gamma, beta, Wf1, bf1, 
             nc.vector.quantize_mx(out=x_codes[:].bitcast(FP8X4), scales=x_scales[:], in_=x_grouped[:])
 
         def prepare_params():
-            params_t = acc[-1][-1][:].bitcast(BF16).rearrange("p (i n) -> p i n", i=TILES)
-            for i in range(TILES):
-                nc.tensor.transpose(params_t[:, i, :], rows_by_tile[:, i * P : (i + 1) * P], ident_bf16[:])
-            nc.vector.tensor_copy(out=params[:], in_=params_t[:, :, :param_rows])
+            params_t = acc[-1][-1][:, : PACK * P // 2].bitcast(BF16).rearrange("p (t n) -> p t n", t=PACK)
+            for t in range(PACK):
+                nc.tensor.transpose(params_t[:, t, :], rows_by_tile[:, t, :], ident_bf16[:])
+            nc.vector.tensor_copy(out=params[:], in_=params_t[:, :, : 3 * vector_rows])
 
-        def quantise_and_multiply(r):
-            slabs = range(ROUND_SLABS * r, ROUND_SLABS * (r + 1))
-            for s in slabs:
-                quantise_slab(s)
+        def multiply(r):
             if r < NB:
                 stage1(r)
             else:
-                for s in slabs:
+                for s in range(ROUND_SLABS * r, ROUND_SLABS * (r + 1)):
                     stage2(s - W_SLABS)
 
         def run_round(r):
             first = ROUND_SLABS * r
             vector_cols = BASE_COLS
             if live(r - 2):
-                vector_cols += RELU_SQUARES_COLS
+                vector_cols += RELU_COLS
             if live(r - 3):
-                vector_cols -= NORMALISE_COLS
+                vector_cols += SQUARES_COLS
             if live(r - 4):
+                vector_cols -= NORMALISE_COLS
+            if live(r - 5):
                 vector_cols -= FUSED_COLS
 
-            relu_and_sums(r - 2)
-            standard_deviation(r - 3)
-            quantise_and_multiply(r - 1)
-
+            standard_deviation(r - 4)
+            quantise_slab(first - 2)
             regroup_slab(first, vector_cols)
-            reciprocal_std(r - 3)
-            negative_mean(r - 2)
+            reciprocal_std(r - 4)
+            quantise_slab(first - 1)
+            gain(r - 4)
             regroup_slab(first + 1, vector_cols)
             load_slab(first + RAW_BUFS)
             load_slab(first + RAW_BUFS + 1)
-            squares(r - 2)
-
-            gain(r - 3)
-            regroup_fused(r - 4, 0)
-            negative_mean_times_gain(r - 3)
-            regroup_fused(r - 4, 1)
-            shift(r - 3)
-            normalise(r - 3)
-            quantise_fused(r - 4)
+            relu_and_sums(r - 2)
+            multiply(r - 1)
             interleave_on_tensor(first + 2)
             interleave_on_tensor(first + 3)
+
+            negative_mean_times_gain(r - 4)
+            regroup_fused(r - 5, 0)
+            shift(r - 4)
+            regroup_fused(r - 5, 1)
+            squares(r - 3)
+            negative_mean(r - 2)
+            normalise(r - 4)
+            quantise_fused(r - 5)
 
         def store(nt):
             cols = slice(nt * N_TILE, (nt + 1) * N_TILE)
@@ -399,16 +422,16 @@ def tile_extremeoptimizationlayer_pa_kernel(tc, x, W, b, gamma, beta, Wf1, bf1, 
                 nc.sync.dma_start(out=out[bt * P : (bt + 1) * P, cols], in_=result[:])
 
         def first_round():
-            piece = DO // HEAD_PIECES
             for s, scalar_pieces in ((0, (1,)), (1, (0, 1))):
                 for i in range(HEAD_PIECES):
                     copy = nc.scalar.copy if i in scalar_pieces else nc.vector.tensor_copy
-                    regroup(copy, s, i * piece, (i + 1) * piece)
-                load_slab(s + RAW_BUFS)
+                    regroup(copy, s, i * HEAD_COLS, (i + 1) * HEAD_COLS)
 
         def last_round():
-            quantise_and_multiply(ROUNDS - 2)
             slabs = range(SLABS - ROUND_SLABS, SLABS)
+            for s in slabs:
+                quantise_slab(s - ROUND_SLABS)
+            multiply(ROUNDS - 2)
             halves = [(nt * N_TILE, (nt + 1) * N_TILE) for nt in range(DO // N_TILE)]
             for first, last in halves:
                 for s in slabs:

@@ -390,6 +390,7 @@ def tile_extremeoptimizationlayer_pa_kernel(tc, x, W, b, gamma, beta, Wf1, bf1, 
             if live(r - 5):
                 vector_cols -= FUSED_COLS
 
+            interleave_on_tensor(first + 1)
             standard_deviation(r - 4)
             quantise_slab(first - 2)
             regroup_slab(first, vector_cols)
@@ -402,7 +403,6 @@ def tile_extremeoptimizationlayer_pa_kernel(tc, x, W, b, gamma, beta, Wf1, bf1, 
             relu_and_sums(r - 2)
             multiply(r - 1)
             interleave_on_tensor(first + 2)
-            interleave_on_tensor(first + 3)
 
             negative_mean_times_gain(r - 4)
             regroup_fused(r - 5, 0)
@@ -443,12 +443,11 @@ def tile_extremeoptimizationlayer_pa_kernel(tc, x, W, b, gamma, beta, Wf1, bf1, 
                     stage2(s - W_SLABS, (nt,))
                 store(nt)
 
+        ctx.enter_context(tc.manual_schedule(engines={mybir.EngineType.PE}))
         first_round()
         prepare_x()
-        interleave_on_tensor(2)
-        interleave_on_tensor(3)
-        run_round(1)
         prepare_params()
-        for r in range(2, ROUNDS - 1):
+        interleave_on_tensor(ROUND_SLABS)
+        for r in range(1, ROUNDS - 1):
             run_round(r)
         last_round()

@@ -37,7 +37,8 @@ NORMALISE_COLS = 128
 FUSED_COLS = 128
 TENSOR_COLS = 256
 TENSOR_SLABS = range(2, 27)
-TENSOR_SLABS_IN_ACC = 20
+STAGE2_SLABS = 20
+STAGE1_BANKS = 6
 ALONE_COLS = 64
 HEAD_PIECES = 4
 HEAD_COLS = DO // HEAD_PIECES
@@ -55,8 +56,7 @@ def tile_extremeoptimizationlayer_pa_kernel(tc, x, W, b, gamma, beta, Wf1, bf1, 
         a_pool = ctx.enter_context(tc.tile_pool(name="a", bufs=3))
         unused_pool = ctx.enter_context(tc.tile_pool(name="unused", bufs=1))
         result_pool = ctx.enter_context(tc.tile_pool(name="result", bufs=4))
-        psum_h = ctx.enter_context(tc.psum_pool(name="psum_h", bufs=4))
-        psum_acc = ctx.enter_context(tc.psum_pool(name="psum_acc", bufs=1))
+        psum = ctx.enter_context(tc.psum_pool(name="psum", bufs=1))
 
         raw_of = {}
         pieces_of = {}
@@ -111,10 +111,8 @@ def tile_extremeoptimizationlayer_pa_kernel(tc, x, W, b, gamma, beta, Wf1, bf1, 
         def interleave_on_tensor(s):
             if s not in TENSOR_SLABS:
                 return
-            if s < TENSOR_SLABS_IN_ACC:
-                bank = acc[s % 2][s // 2 % 2][:].bitcast(BF16).rearrange("p (c k) -> p c k", k=PACK)
-            else:
-                bank = psum_h.tile([P, TENSOR_COLS, PACK], BF16, name="h")
+            bank = banks[s % 4] if s >= STAGE2_SLABS else banks[-2 + s % 2]
+            bank = bank[:].bitcast(BF16).rearrange("p (c k) -> p c k", k=PACK)
             bank_of[s] = bank
             cols = N_TILE // PACK
             for first in range(0, TENSOR_COLS, cols):
@@ -164,7 +162,7 @@ def tile_extremeoptimizationlayer_pa_kernel(tc, x, W, b, gamma, beta, Wf1, bf1, 
         def stage1(br):
             h_of[br] = []
             for pair in range(TILES // 2):
-                h = psum_h.tile([P, 2, B], F32, name="h")
+                h = banks[(TILES // 2 * br + pair) % STAGE1_BANKS].rearrange("p (i n) -> p i n", n=B)
                 for half in range(2):
                     j, t = divmod(2 * pair + half, PACK)
                     cols = slice((GROUPS * t + j) * P, (GROUPS * t + j + 1) * P)
@@ -347,17 +345,15 @@ def tile_extremeoptimizationlayer_pa_kernel(tc, x, W, b, gamma, beta, Wf1, bf1, 
         params = const.tile([P, PACK, 3 * vector_rows], F32, name="params")
         f_codes = const.tile([P, F // K_PASS, B], U32, name="f_codes", align_bytes=64)
         f_scales = const.tile([P, F // K_PASS, B], U8, name="f_scales", align_bytes=64)
-        acc = [
-            [psum_acc.tile([P, N_TILE], F32, name="acc%d%d" % (bt, nt)) for nt in range(DO // N_TILE)]
-            for bt in range(B // P)
-        ]
+        banks = [psum.tile([P, N_TILE], F32, name="bank%d" % i) for i in range(8)]
+        acc = [banks[4:6], banks[6:8]]
 
         def prepare_x():
             x_words = x_sb[:].bitcast(F32).rearrange("p (bt c q u) -> p bt c q u", bt=B // P, c=W_PASSES, q=P)
             x_grouped_words = x_grouped[:].bitcast(F32).rearrange("p (c n u) -> p c n u", c=W_PASSES, n=B)
             x_t = []
             for c in range(W_PASSES):
-                x_t.append(psum_h.tile([P, 2, B], F32, name="h"))
+                x_t.append(banks[c].rearrange("p (u n) -> p u n", n=B))
                 for u in range(2):
                     for bt in range(B // P):
                         nc.tensor.transpose(x_t[c][:, u, bt * P : (bt + 1) * P], x_words[:, bt, c, :, u], ident_f32[:])
@@ -366,7 +362,7 @@ def tile_extremeoptimizationlayer_pa_kernel(tc, x, W, b, gamma, beta, Wf1, bf1, 
             nc.vector.quantize_mx(out=x_codes[:].bitcast(FP8X4), scales=x_scales[:], in_=x_grouped[:])
 
         def prepare_params():
-            params_t = acc[-1][-1][:, : PACK * P // 2].bitcast(BF16).rearrange("p (t n) -> p t n", t=PACK)
+            params_t = banks[-1][:, : PACK * P // 2].bitcast(BF16).rearrange("p (t n) -> p t n", t=PACK)
             for t in range(PACK):
                 nc.tensor.transpose(params_t[:, t, :], rows_by_tile[:, t, :], ident_bf16[:])
             nc.vector.tensor_copy(out=params[:], in_=params_t[:, :, : 3 * vector_rows])

from contextlib import ExitStack

import concourse.mybir as mybir
from concourse.masks import make_identity

F32 = mybir.dt.float32
BF16 = mybir.dt.bfloat16
U32 = mybir.dt.uint32
U8 = mybir.dt.uint8
FP8X4 = mybir.dt.float8_e4m3fn_x4
ACT = mybir.ActivationFunctionType
ALU = mybir.AluOpType

P = 128
PACK = 4
K_PASS = P * PACK
NB, DI, DO, B = 8, 1024, 1024, 256
F = NB * DO
EPS = 1e-5
FLOPS = 2 * B * DI * F + 2 * B * F * DO

TILES = DO // P
GROUPS = DO // K_PASS
W_PASSES = DI // K_PASS
W_SLABS = NB * W_PASSES
SLABS = W_SLABS + F // K_PASS
ROUND_SLABS = 2
ROUNDS = SLABS // ROUND_SLABS
N_TILE = 512
RUN = 4

RAW_BUFS = 9
BASE_COLS = 448
RELU_COLS = 192
SQUARES_COLS = 192
NORMALISE_COLS = 128
FUSED_COLS = 128
TENSOR_COLS = 256
TENSOR_SLABS = range(2, 27)
STAGE2_SLABS = 20
STAGE1_BANKS = 6
ALONE_COLS = 64
HEAD_PIECES = 4
HEAD_COLS = DO // HEAD_PIECES
LAST_COLS = 128


def tile_extremeoptimizationlayer_pa_kernel(tc, x, W, b, gamma, beta, Wf1, bf1, out):
    nc = tc.nc
    with ExitStack() as ctx:
        const = ctx.enter_context(tc.tile_pool(name="const", bufs=1))
        raw_pool = ctx.enter_context(tc.tile_pool(name="raw", bufs=RAW_BUFS))
        slab_pool = ctx.enter_context(tc.tile_pool(name="slab", bufs=2 * ROUND_SLABS))
        branch_pool = ctx.enter_context(tc.tile_pool(name="branch", bufs=2))
        stat_pool = ctx.enter_context(tc.tile_pool(name="stat", bufs=4))
        a_pool = ctx.enter_context(tc.tile_pool(name="a", bufs=3))
        unused_pool = ctx.enter_context(tc.tile_pool(name="unused", bufs=1))
        result_pool = ctx.enter_context(tc.tile_pool(name="result", bufs=4))
        psum = ctx.enter_context(tc.psum_pool(name="psum", bufs=1))

        raw_of = {}
        pieces_of = {}
        grouped_of = {}
        codes_of = {}
        bank_of = {}
        h_of = {}
        bn = {}

        def rows_of_w(s):
            return W[s // W_PASSES, (s % W_PASSES) * K_PASS : (s % W_PASSES + 1) * K_PASS, :]

        def load_head_slab(s):
            pieces_of[s] = []
            for i in range(HEAD_PIECES):
                piece = const.tile([P, PACK, HEAD_COLS], BF16, name="piece%d_%d" % (s, i))
                cols = slice(i * HEAD_COLS, (i + 1) * HEAD_COLS)
                nc.sync.dma_start(out=piece[:], in_=rows_of_w(s)[:, cols].rearrange("(p t) w -> p t w", t=PACK))
                pieces_of[s].append(piece)

        def load_slab(s):
            if s >= SLABS:
                return
            raw = raw_pool.tile([P, PACK, DO], BF16, name="raw")
            if s < W_SLABS:
                nc.sync.dma_start(out=raw[:], in_=rows_of_w(s).rearrange("(p t) w -> p t w", t=PACK))
            else:
                g = s - W_SLABS
                rows = Wf1[g * K_PASS : (g + 1) * K_PASS, :].rearrange("(q t i) w -> t q i w", t=PACK, i=RUN)
                for t in range(PACK):
                    nc.sync.dma_start(out=raw[:, t, :], in_=rows[t])
            raw_of[s] = raw

        def regroup(engine_copy, s, first, last):
            if s not in grouped_of:
                grouped = slab_pool.tile([P, DO, PACK], BF16, name="grouped", align_bytes=64)
                grouped_of[s] = grouped
            grouped = grouped_of[s]
            if s in pieces_of:
                src = pieces_of[s][first // HEAD_COLS]
            else:
                src = raw_of[s][:, :, first:last]
            if s < W_SLABS:
                src = src.rearrange("p k (q t i) -> p q t k i", t=PACK, i=RUN)
                dst = grouped.rearrange("p (t q i) k -> p q t k i", t=PACK, i=RUN)
                dst = dst[:, first // (PACK * RUN) : last // (PACK * RUN)]
            else:
                src = src.rearrange("p k (c i) -> p c k i", i=RUN)
                dst = grouped[:, first:last, :].rearrange("p (c i) k -> p c k i", i=RUN)
            engine_copy(out=dst, in_=src)

        def interleave_on_tensor(s):
            if s not in TENSOR_SLABS:
                return
            bank = banks[s % 4] if s >= STAGE2_SLABS else banks[-2 + s % 2]
            bank = bank[:].bitcast(BF16).rearrange("p (c k) -> p c k", k=PACK)
            bank_of[s] = bank
            cols = N_TILE // PACK
            for first in range(0, TENSOR_COLS, cols):
                nc.tensor.matmul(
                    out=bank[:, first : first + cols, :].rearrange("p c k -> p k c"),
                    lhsT=ident_bf16[:],
                    rhs=raw_of[s][:, :, DO - TENSOR_COLS + first : DO - TENSOR_COLS + first + cols],
                    start=True,
                    stop=True,
                )

        def copy_from_tensor(s):
            first = DO - TENSOR_COLS
            if s < W_SLABS:
                src = bank_of[s].rearrange("p (q t i) k -> p q t (i k)", t=PACK, i=RUN)
                dst = grouped_of[s].rearrange("p (t q i) k -> p q t (i k)", t=PACK, i=RUN)[:, first // (PACK * RUN) :]
            else:
                src = bank_of[s].rearrange("p c k -> p (c k)")
                dst = grouped_of[s][:, first:, :].rearrange("p c k -> p (c k)")
            nc.scalar.copy(out=dst.bitcast(F32), in_=src.bitcast(F32))

        def regroup_slab(s, vector_cols):
            if s not in TENSOR_SLABS:
                vector_cols += ALONE_COLS
                regroup(nc.vector.tensor_copy, s, 0, vector_cols)
                regroup(nc.scalar.copy, s, vector_cols, DO)
                return
            last = DO - TENSOR_COLS
            vector_cols = min(vector_cols, last)
            regroup(nc.vector.tensor_copy, s, 0, vector_cols)
            if vector_cols < last:
                regroup(nc.scalar.copy, s, vector_cols, last)
            copy_from_tensor(s)

        def quantise_slab(s, first=0, last=DO):
            if s not in codes_of:
                codes = slab_pool.tile([P, DO], U32, name="codes", align_bytes=64)
                scales = slab_pool.tile([P, DO], U8, name="scales", align_bytes=64)
                codes_of[s] = (codes, scales)
            codes, scales = codes_of[s]
            nc.vector.quantize_mx(
                out=codes[:, first:last].bitcast(FP8X4),
                scales=scales[:, first:last],
                in_=grouped_of[s][:, first:last, :].rearrange("p w t -> p (w t)"),
            )

        def stage1(br):
            h_of[br] = []
            for pair in range(TILES // 2):
                h = banks[(TILES // 2 * br + pair) % STAGE1_BANKS].rearrange("p (i n) -> p i n", n=B)
                for half in range(2):
                    j, t = divmod(2 * pair + half, PACK)
                    cols = slice((GROUPS * t + j) * P, (GROUPS * t + j + 1) * P)
                    for c in range(W_PASSES):
                        codes, scales = codes_of[W_PASSES * br + c]
                        nc.tensor.matmul_mx(
                            out=h[:, half, :],
                            lhsT=codes[:, cols].bitcast(FP8X4),
                            lhsT_scale=scales[:, cols],
                            rhs=x_codes[:, c * B : (c + 1) * B].bitcast(FP8X4),
                            rhs_scale=x_scales[:, c * B : (c + 1) * B],
                            start=(c == 0),
                            stop=(c == W_PASSES - 1),
                        )
                h_of[br].append(h)

        def stage2(g, column_tiles=range(DO // N_TILE)):
            codes, scales = codes_of[W_SLABS + g]
            for bt in range(B // P):
                rows = slice(bt * P, (bt + 1) * P)
                for nt in column_tiles:
                    cols = slice(nt * N_TILE, (nt + 1) * N_TILE)
                    nc.tensor.matmul_mx(
                        out=acc[bt][nt][:],
                        lhsT=f_codes[:, g, rows].bitcast(FP8X4),
                        lhsT_scale=f_scales[:, g, rows],
                        rhs=codes[:, cols].bitcast(FP8X4),
                        rhs_scale=scales[:, cols],
                        start=(g == 0),
                        stop=(g == F // K_PASS - 1),
                    )

        def live(br):
            return 0 <= br < NB

        def stat_tile(name, br):
            bn[(name, br)] = stat_pool.tile([P, TILES], F32, name=name)
            return bn[(name, br)]

        def by_pass(stat):
            return stat.rearrange("p (j t) -> p j t", t=PACK)

        def branch_params(vector, br):
            first = GROUPS * (NB * vector + br)
            return params[:, :, first : first + GROUPS].rearrange("p t j -> p j t")

        def relu_and_sums(br):
            if not live(br):
                return
            a = a_pool.tile([P, TILES, B], F32, name="a")
            bn[("a", br)] = a
            sums = stat_tile("sums", br)
            for i in range(TILES):
                nc.scalar.activation(
                    out=a[:, i, :],
                    in_=h_of[br][i // 2][:, i % 2, :],
                    func=ACT.Relu,
                    bias=params[:, i % PACK, GROUPS * br + i // PACK : GROUPS * br + i // PACK + 1],
                    accum_out=sums[:, i : i + 1],
                )

        def negative_mean(br):
            if live(br):
                nc.scalar.mul(out=stat_tile("neg_mean", br)[:], in_=bn[("sums", br)][:], mul=-1.0 / B)

        def squares(br):
            if not live(br):
                return
            unused = unused_pool.tile([P, TILES, B], BF16, name="unused")
            sumsq = stat_tile("sumsq", br)
            for i in range(TILES):
                nc.scalar.activation(
                    out=unused[:, i, :],
                    in_=bn[("a", br)][:, i, :],
                    func=ACT.Square,
                    bias=bn[("neg_mean", br)][:, i : i + 1],
                    accum_out=sumsq[:, i : i + 1],
                )

        def standard_deviation(br):
            if live(br):
                nc.scalar.activation(
                    out=stat_tile("std", br)[:], in_=bn[("sumsq", br)][:], func=ACT.Sqrt, bias=eps_col[:], scale=1.0 / B
                )

        def reciprocal_std(br):
            if live(br):
                nc.vector.reciprocal(out=stat_tile("rstd", br)[:], in_=bn[("std", br)][:])

        def gain(br):
            if live(br):
                nc.vector.tensor_mul(
                    out=by_pass(stat_tile("gain", br)), in0=by_pass(bn[("rstd", br)]), in1=branch_params(1, br)
                )

        def negative_mean_times_gain(br):
            if live(br):
                nc.vector.tensor_mul(out=stat_tile("moved", br)[:], in0=bn[("neg_mean", br)][:], in1=bn[("gain", br)][:])

        def shift(br):
            if live(br):
                nc.vector.tensor_add(
                    out=by_pass(stat_tile("shift", br)), in0=by_pass(bn[("moved", br)]), in1=branch_params(2, br)
                )

        def normalise(br):
            if not live(br):
                return
            normed = branch_pool.tile([P, TILES, B], BF16, name="normed")
            bn[("normed", br)] = normed
            for i in range(TILES):
                nc.vector.tensor_scalar(
                    out=normed[:, i, :],
                    in0=bn[("a", br)][:, i, :],
                    scalar1=bn[("gain", br)][:, i : i + 1],
                    scalar2=bn[("shift", br)][:, i : i + 1],
                    op0=ALU.mult,
                    op1=ALU.add,
                )

        def regroup_fused(br, j):
            if not live(br):
                return
            if j == 0:
                bn[("f_grouped", br)] = branch_pool.tile([P, GROUPS, B, PACK], BF16, name="f_grouped", align_bytes=64)
            nc.vector.tensor_copy(
                out=bn[("f_grouped", br)][:, j].rearrange("p (c i) t -> p c t i", i=RUN),
                in_=bn[("normed", br)][:, PACK * j : PACK * (j + 1), :].rearrange("p t (c i) -> p c t i", i=RUN),
            )

        def quantise_fused(br):
            if live(br):
                passes = slice(GROUPS * br, GROUPS * (br + 1))
                nc.vector.quantize_mx(
                    out=f_codes[:, passes, :].rearrange("p g n -> p (g n)").bitcast(FP8X4),
                    scales=f_scales[:, passes, :].rearrange("p g n -> p (g n)"),
                    in_=bn[("f_grouped", br)].rearrange("p g n t -> p (g n t)"),
                )

        x_sb = const.tile([P, (B // P) * DI], BF16, name="x_sb")
        for s in range(ROUND_SLABS):
            load_head_slab(s)
        nc.sync.dma_start(
            out=x_sb.rearrange("p (bt k) -> p bt k", k=DI), in_=x.rearrange("(bt p) k -> p bt k", p=P)
        )
        for s in range(ROUND_SLABS, ROUND_SLABS + RAW_BUFS):
            load_slab(s)
        bias_all = const.tile([P, DO], BF16, name="bias_all")
        nc.sync.dma_start(out=bias_all[:], in_=bf1.partition_broadcast(P))

        vector_rows = GROUPS * NB
        rows = const.tile([P // 2, K_PASS], BF16, name="rows")
        for v, vectors in enumerate((b, gamma, beta, b)):
            nc.scalar.dma_start(
                out=rows[vector_rows * v : vector_rows * (v + 1), :], in_=vectors.rearrange("k (j f) -> (k j) f", j=GROUPS)
            )
        eps_col = const.tile([P, 1], F32, name="eps_col")
        nc.vector.memset(eps_col[:], EPS)
        first_sqrt = const.tile([P, 1], F32, name="first_sqrt")
        nc.scalar.activation(out=first_sqrt[:], in_=eps_col[:], func=ACT.Sqrt)

        ident_f32 = const.tile([P, P], F32, name="ident_f32")
        make_identity(nc, ident_f32[:])
        ident_bf16 = const.tile([P, P], BF16, name="ident_bf16")
        make_identity(nc, ident_bf16[:])

        x_grouped = const.tile([P, W_PASSES * B * PACK], BF16, name="x_grouped", align_bytes=64)
        x_codes = const.tile([P, W_PASSES * B], U32, name="x_codes", align_bytes=64)
        x_scales = const.tile([P, W_PASSES * B], U8, name="x_scales", align_bytes=64)
        rows_by_tile = const.tile([P, PACK, P], BF16, name="rows_by_tile")
        nc.gpsimd.memset(rows_by_tile[P // 2 :, :, :], 0.0)
        nc.gpsimd.tensor_scalar(
            out=rows_by_tile[: P // 2].rearrange("p t (q i) -> p q t i", i=RUN),
            in0=rows.rearrange("p (q t i) -> p q t i", t=PACK, i=RUN),
            scalar1=1.0,
            scalar2=0.0,
            op0=ALU.mult,
            op1=ALU.add,
        )
        params = const.tile([P, PACK, 3 * vector_rows], F32, name="params")
        f_codes = const.tile([P, F // K_PASS, B], U32, name="f_codes", align_bytes=64)
        f_scales = const.tile([P, F // K_PASS, B], U8, name="f_scales", align_bytes=64)
        banks = [psum.tile([P, N_TILE], F32, name="bank%d" % i) for i in range(8)]
        acc = [banks[4:6], banks[6:8]]

        def prepare_x():
            x_words = x_sb[:].bitcast(F32).rearrange("p (bt c q u) -> p bt c q u", bt=B // P, c=W_PASSES, q=P)
            x_grouped_words = x_grouped[:].bitcast(F32).rearrange("p (c n u) -> p c n u", c=W_PASSES, n=B)
            x_t = []
            for c in range(W_PASSES):
                x_t.append(banks[c].rearrange("p (u n) -> p u n", n=B))
                for u in range(2):
                    for bt in range(B // P):
                        nc.tensor.transpose(x_t[c][:, u, bt * P : (bt + 1) * P], x_words[:, bt, c, :, u], ident_f32[:])
            nc.vector.tensor_copy(out=x_grouped_words[:, 0], in_=x_t[0].rearrange("p u n -> p n u"))
            nc.scalar.copy(out=x_grouped_words[:, 1], in_=x_t[1].rearrange("p u n -> p n u"))
            nc.vector.quantize_mx(out=x_codes[:].bitcast(FP8X4), scales=x_scales[:], in_=x_grouped[:])

        def prepare_params():
            params_t = banks[-1][:, : PACK * P // 2].bitcast(BF16).rearrange("p (t n) -> p t n", t=PACK)
            for t in range(PACK):
                nc.tensor.transpose(params_t[:, t, :], rows_by_tile[:, t, :], ident_bf16[:])
            nc.vector.tensor_copy(out=params[:], in_=params_t[:, :, : 3 * vector_rows])

        def multiply(r):
            if r < NB:
                stage1(r)
            else:
                for s in range(ROUND_SLABS * r, ROUND_SLABS * (r + 1)):
                    stage2(s - W_SLABS)

        def run_round(r):
            first = ROUND_SLABS * r
            vector_cols = BASE_COLS
            if live(r - 2):
                vector_cols += RELU_COLS
            if live(r - 3):
                vector_cols += SQUARES_COLS
            if live(r - 4):
                vector_cols -= NORMALISE_COLS
            if live(r - 5):
                vector_cols -= FUSED_COLS

            interleave_on_tensor(first + 1)
            standard_deviation(r - 4)
            quantise_slab(first - 2)
            regroup_slab(first, vector_cols)
            reciprocal_std(r - 4)
            quantise_slab(first - 1)
            gain(r - 4)
            regroup_slab(first + 1, vector_cols)
            load_slab(first + RAW_BUFS)
            load_slab(first + RAW_BUFS + 1)
            relu_and_sums(r - 2)
            multiply(r - 1)
            interleave_on_tensor(first + 2)

            negative_mean_times_gain(r - 4)
            regroup_fused(r - 5, 0)
            shift(r - 4)
            regroup_fused(r - 5, 1)
            squares(r - 3)
            negative_mean(r - 2)
            normalise(r - 4)
            quantise_fused(r - 5)

        def store(nt):
            cols = slice(nt * N_TILE, (nt + 1) * N_TILE)
            for bt in range(B // P):
                result = result_pool.tile([P, N_TILE], F32, name="result")
                nc.vector.tensor_tensor(out=result[:], in0=acc[bt][nt][:], in1=bias_all[:, cols], op=ALU.add)
                nc.scalar.activation(out=result[:], in_=result[:], func=ACT.Relu)
                nc.sync.dma_start(out=out[bt * P : (bt + 1) * P, cols], in_=result[:])

        def first_round():
            for s, scalar_pieces in ((0, (1,)), (1, (0, 1))):
                for i in range(HEAD_PIECES):
                    copy = nc.scalar.copy if i in scalar_pieces else nc.vector.tensor_copy
                    regroup(copy, s, i * HEAD_COLS, (i + 1) * HEAD_COLS)

        def last_round():
            slabs = range(SLABS - ROUND_SLABS, SLABS)
            for s in slabs:
                quantise_slab(s - ROUND_SLABS)
            multiply(ROUNDS - 2)
            halves = [(nt * N_TILE, (nt + 1) * N_TILE) for nt in range(DO // N_TILE)]
            for first, last in halves:
                for s in slabs:
                    regroup(nc.vector.tensor_copy, s, first, first + LAST_COLS)
                    regroup(nc.scalar.copy, s, first + LAST_COLS, last)
            for nt, (first, last) in enumerate(halves):
                for s in slabs:
                    quantise_slab(s, first, last)
                    stage2(s - W_SLABS, (nt,))
                store(nt)

        ctx.enter_context(tc.manual_schedule(engines={mybir.EngineType.PE}))
        first_round()
        prepare_x()
        prepare_params()
        interleave_on_tensor(ROUND_SLABS)
        for r in range(1, ROUNDS - 1):
            run_round(r)
        last_round()
